import numpy as np
import ml_dtypes

BF16 = ml_dtypes.bfloat16


def bf(x):
    return np.asarray(x, np.float32).astype(BF16)


def f32(x):
    return np.asarray(x, np.float32)


def f64(x):
    return np.asarray(x).astype(np.float64)


def striped(idx):
    return np.tile(idx.reshape(-1, 16).T, (8, 1))


D, S, N, R, T = 128, 4096, 1024, 4, 256


def sigmoid(v):
    return 1.0 / (1.0 + np.exp(-v))


def setup_inputs():
    mu = 0.5 * np.random.standard_normal((D, 1))
    return {
        "table": bf(mu + np.random.standard_normal((D, S))),
        "w_word": bf(1.5 * np.random.standard_normal((D, D)) / np.sqrt(D)),
        "w_sent": bf(2.0 * np.random.standard_normal((D, D)) / np.sqrt(D)),
        "w_forget": bf(2.0 * np.random.standard_normal((D, D)) / np.sqrt(D)),
        "b_word": f32(np.random.standard_normal((D, 1))),
        "b_forget": f32(0.5 * np.random.standard_normal((D, 1))),
        "offs": striped(np.random.permutation(np.tile(np.arange(S), 2))[:N]),
    }


def reference(table, w_word, w_sent, w_forget, b_word, b_forget, offs):
    idx = offs[:16].T.reshape(-1)
    e = f64(table)[:, idx]
    p = (f64(w_word).T @ e).reshape(D, R, T)
    q = (f64(w_sent).T @ e).reshape(D, R, T).mean(axis=2, keepdims=True)
    a = (f64(w_forget).T @ e).reshape(D, R, T).mean(axis=2, keepdims=True)
    f = sigmoid(a + f64(b_forget)[:, :, None])
    x = np.exp(sigmoid(p + q + f64(b_word)[:, :, None]))
    share = x / x.mean(axis=2, keepdims=True)
    return (e.reshape(D, R, T) * (share + f)).reshape(D, N)

@@ -1,0 +1,106 @@
+import concourse.mybir as mybir
+from concourse.masks import make_identity
+
+D = 128
+S = 4096
+N = 1024
+T = 256
+R = N // T
+PAIR = 2
+PAIRS = R // PAIR
+HALF_MEAN = 0.5 / T
+FLOPS = 3 * 2 * D * D * N
+
+BF16, F32, U16 = mybir.dt.bfloat16, mybir.dt.float32, mybir.dt.uint16
+MULT, ADD = mybir.AluOpType.mult, mybir.AluOpType.add
+TANH, EXP = mybir.ActivationFunctionType.Tanh, mybir.ActivationFunctionType.Exp
+COPY = mybir.ActivationFunctionType.Copy
+X_AXIS = mybir.AxisListType.X
+
+
+def tile_slstm_kernel(tc, table, w_word, w_sent, w_forget, b_word, b_forget, offs, out):
+    nc = tc.nc
+    with (
+        tc.tile_pool(name="held", bufs=1) as held,
+        tc.tile_pool(name="scratch", bufs=2) as scratch,
+        tc.psum_pool(name="psum", bufs=2) as psum,
+    ):
+        words = held.tile([D, S], BF16, name="words")
+        nc.sync.dma_start(words[:], table)
+        offsets = held.tile([D, N // 16], U16, name="offsets")
+        nc.sync.dma_start(offsets[:], offs)
+        sent_w = held.tile([D, D], BF16, name="sent_w")
+        nc.scalar.dma_start(sent_w[:], w_sent)
+        word_b = held.tile([D, 1], F32, name="word_b")
+        nc.scalar.dma_start(word_b[:], b_word)
+        word_w = held.tile([D, D], BF16, name="word_w")
+        nc.scalar.dma_start(word_w[:], w_word)
+        forget_w = held.tile([D, D], BF16, name="forget_w")
+        nc.sync.dma_start(forget_w[:], w_forget)
+        forget_b = held.tile([D, 1], F32, name="forget_b")
+        nc.sync.dma_start(forget_b[:], b_forget)
+        identity = held.tile([D, D], BF16, name="identity")
+        make_identity(nc, identity[:])
+
+        primer = held.tile([D, 1], F32, name="primer")
+        nc.vector.memset(primer[:], 0.0)
+        primed = held.tile([D, 1], F32, name="primed")
+        nc.scalar.activation(primed[:], primer[:], TANH)
+
+        half_word_b = held.tile([D, 1], F32, name="half_word_b")
+        nc.vector.tensor_scalar(half_word_b[:], word_b[:], 0.5, None, op0=MULT)
+        half_forget_b = held.tile([D, 1], F32, name="half_forget_b")
+        nc.vector.tensor_scalar(half_forget_b[:], forget_b[:], 0.5, None, op0=MULT)
+
+        def looked_up(first_sentence, sentences):
+            first = first_sentence * T // 16
+            return words[:].indirect(offsets[:, first : first + sentences * T // 16])
+
+        gate = [held.tile([D, T], F32, name=f"gate{r}") for r in range(R)]
+        x = [held.tile([D, T], F32, name=f"x{r}") for r in range(R)]
+        x_sum = [held.tile([D, 1], F32, name=f"x_sum{r}") for r in range(R)]
+        x_sum_inv = [held.tile([D, 1], F32, name=f"x_sum_inv{r}") for r in range(R)]
+        share = [held.tile([D, T], F32, name=f"share{r}") for r in range(R)]
+
+        def make_share(r):
+            nc.scalar.activation(x[r][:], gate[r][:], EXP, scale=0.5, accum_out=x_sum[r][:])
+            nc.vector.reciprocal(x_sum_inv[r][:], x_sum[r][:])
+            nc.vector.tensor_scalar(share[r][:], x[r][:], x_sum_inv[r][:], float(T), op0=MULT, op1=MULT)
+
+        for r in range(R):
+            sent_proj = psum.tile([D, T], F32, name="sent_proj", tag="summed")
+            nc.tensor.matmul(sent_proj[:], sent_w[:], looked_up(r, 1), start=True, stop=True)
+            word_proj = psum.tile([D, T], F32, name="word_proj", tag="word_proj")
+            nc.tensor.matmul(word_proj[:], word_w[:], looked_up(r, 1), start=True, stop=True)
+
+            scaled = scratch.tile([D, T], F32, name="scaled")
+            gate_bias = held.tile([D, 1], F32, name=f"gate_bias{r}")
+            nc.vector.tensor_scalar(
+                scaled[:], sent_proj[:], HALF_MEAN, half_word_b[:],
+                op0=MULT, op1=ADD, accum_out=gate_bias[:],
+            )
+            nc.scalar.activation(gate[r][:], word_proj[:], TANH, bias=gate_bias[:], scale=0.5)
+            if r > 0:
+                make_share(r - 1)
+        make_share(R - 1)
+
+        f = [held.tile([D, PAIR], F32, name=f"f{h}") for h in range(PAIRS)]
+        for h in range(PAIRS):
+            forget_proj = psum.tile([D, PAIR * T], F32, name="forget_proj", tag="summed")
+            nc.tensor.matmul(forget_proj[:], forget_w[:], looked_up(h * PAIR, PAIR), start=True, stop=True)
+            a_sum = held.tile([D, PAIR], F32, name=f"a_sum{h}")
+            nc.vector.reduce_sum(a_sum[:], forget_proj[:].rearrange("p (r t) -> p r t", t=T), axis=X_AXIS)
+            f_tanh = held.tile([D, PAIR], F32, name=f"f_tanh{h}")
+            nc.scalar.activation(f_tanh[:], a_sum[:], TANH, bias=half_forget_b[:], scale=HALF_MEAN)
+            nc.scalar.activation(f[h][:], f_tanh[:], COPY, bias=0.5, scale=0.5)
+
+        result = held.tile([D, N], F32, name="result")
+        for r in range(R):
+            h, s = divmod(r, PAIR)
+            picked = psum.tile([D, T], F32, name="picked", tag="picked", bufs=R)
+            nc.tensor.matmul(picked[:], identity[:], looked_up(r, 1), start=True, stop=True)
+            nc.vector.scalar_tensor_tensor(
+                result[:, r * T : (r + 1) * T], share[r][:], f[h][:, s : s + 1], picked[:],
+                op0=ADD, op1=MULT,
+            )
+            nc.sync.dma_start(out[:, r * T : (r + 1) * T], result[:, r * T : (r + 1) * T])

@@ -31,10 +31,10 @@ def tile_slstm_kernel(tc, table, w_word, w_sent, w_forget, b_word, b_forget, off
         nc.sync.dma_start(offsets[:], offs)
         sent_w = held.tile([D, D], BF16, name="sent_w")
         nc.scalar.dma_start(sent_w[:], w_sent)
-        word_b = held.tile([D, 1], F32, name="word_b")
-        nc.scalar.dma_start(word_b[:], b_word)
         word_w = held.tile([D, D], BF16, name="word_w")
-        nc.scalar.dma_start(word_w[:], w_word)
+        nc.sync.dma_start(word_w[:], w_word)
+        word_b = held.tile([D, 1], F32, name="word_b")
+        nc.sync.dma_start(word_b[:], b_word)
         forget_w = held.tile([D, D], BF16, name="forget_w")
         nc.sync.dma_start(forget_w[:], w_forget)
         forget_b = held.tile([D, 1], F32, name="forget_b")

@@ -9,6 +9,7 @@ R = N // T
 PAIR = 2
 PAIRS = R // PAIR
 HALF_MEAN = 0.5 / T
+HALF_SHARE = 0.5 / T
 FLOPS = 3 * 2 * D * D * N
 
 BF16, F32, U16 = mybir.dt.bfloat16, mybir.dt.float32, mybir.dt.uint16
@@ -34,13 +35,15 @@ def tile_slstm_kernel(tc, table, w_word, w_sent, w_forget, b_word, b_forget, off
         word_w = held.tile([D, D], BF16, name="word_w")
         nc.sync.dma_start(word_w[:], w_word)
         word_b = held.tile([D, 1], F32, name="word_b")
-        nc.sync.dma_start(word_b[:], b_word)
+        nc.scalar.dma_start(word_b[:], b_word)
         forget_w = held.tile([D, D], BF16, name="forget_w")
         nc.sync.dma_start(forget_w[:], w_forget)
         forget_b = held.tile([D, 1], F32, name="forget_b")
-        nc.sync.dma_start(forget_b[:], b_forget)
+        nc.scalar.dma_start(forget_b[:], b_forget)
         identity = held.tile([D, D], BF16, name="identity")
         make_identity(nc, identity[:])
+        scaled_identity = held.tile([D, D], BF16, name="scaled_identity")
+        nc.gpsimd.tensor_scalar(scaled_identity[:], identity[:], float(T), None, op0=MULT)
 
         primer = held.tile([D, 1], F32, name="primer")
         nc.vector.memset(primer[:], 0.0)
@@ -65,7 +68,10 @@ def tile_slstm_kernel(tc, table, w_word, w_sent, w_forget, b_word, b_forget, off
         def make_share(r):
             nc.scalar.activation(x[r][:], gate[r][:], EXP, scale=0.5, accum_out=x_sum[r][:])
             nc.vector.reciprocal(x_sum_inv[r][:], x_sum[r][:])
-            nc.vector.tensor_scalar(share[r][:], x[r][:], x_sum_inv[r][:], float(T), op0=MULT, op1=MULT)
+            if r == R - 1:
+                nc.scalar.activation(share[r][:], x[r][:], COPY, scale=x_sum_inv[r][:])
+            else:
+                nc.vector.tensor_scalar(share[r][:], x[r][:], x_sum_inv[r][:], None, op0=MULT)
 
         for r in range(R):
             sent_proj = psum.tile([D, T], F32, name="sent_proj", tag="summed")
@@ -86,19 +92,20 @@ def tile_slstm_kernel(tc, table, w_word, w_sent, w_forget, b_word, b_forget, off
 
         f = [held.tile([D, PAIR], F32, name=f"f{h}") for h in range(PAIRS)]
         for h in range(PAIRS):
-            forget_proj = psum.tile([D, PAIR * T], F32, name="forget_proj", tag="summed")
-            nc.tensor.matmul(forget_proj[:], forget_w[:], looked_up(h * PAIR, PAIR), start=True, stop=True)
             a_sum = held.tile([D, PAIR], F32, name=f"a_sum{h}")
-            nc.vector.reduce_sum(a_sum[:], forget_proj[:].rearrange("p (r t) -> p r t", t=T), axis=X_AXIS)
+            for s in range(PAIR):
+                forget_proj = psum.tile([D, T], F32, name="forget_proj", tag="summed" if h == 0 else "word_proj")
+                nc.tensor.matmul(forget_proj[:], forget_w[:], looked_up(h * PAIR + s, 1), start=True, stop=True)
+                nc.vector.reduce_sum(a_sum[:, s : s + 1], forget_proj[:], axis=X_AXIS)
             f_tanh = held.tile([D, PAIR], F32, name=f"f_tanh{h}")
             nc.scalar.activation(f_tanh[:], a_sum[:], TANH, bias=half_forget_b[:], scale=HALF_MEAN)
-            nc.scalar.activation(f[h][:], f_tanh[:], COPY, bias=0.5, scale=0.5)
+            nc.scalar.activation(f[h][:], f_tanh[:], COPY, bias=HALF_SHARE, scale=HALF_SHARE)
 
         result = held.tile([D, N], F32, name="result")
         for r in range(R):
             h, s = divmod(r, PAIR)
             picked = psum.tile([D, T], F32, name="picked", tag="picked", bufs=R)
-            nc.tensor.matmul(picked[:], identity[:], looked_up(r, 1), start=True, stop=True)
+            nc.tensor.matmul(picked[:], scaled_identity[:], looked_up(r, 1), start=True, stop=True)
             nc.vector.scalar_tensor_tensor(
                 result[:, r * T : (r + 1) * T], share[r][:], f[h][:, s : s + 1], picked[:],
                 op0=ADD, op1=MULT,

@@ -6,8 +6,7 @@ S = 4096
 N = 1024
 T = 256
 R = N // T
-PAIR = 2
-PAIRS = R // PAIR
+GATE_GROUPS = ((0, 1), (2,), (3,))
 HALF_MEAN = 0.5 / T
 HALF_SHARE = 0.5 / T
 FLOPS = 3 * 2 * D * D * N
@@ -90,24 +89,24 @@ def tile_slstm_kernel(tc, table, w_word, w_sent, w_forget, b_word, b_forget, off
                 make_share(r - 1)
         make_share(R - 1)
 
-        f = [held.tile([D, PAIR], F32, name=f"f{h}") for h in range(PAIRS)]
-        for h in range(PAIRS):
-            a_sum = held.tile([D, PAIR], F32, name=f"a_sum{h}")
-            for s in range(PAIR):
-                forget_proj = psum.tile([D, T], F32, name="forget_proj", tag="summed" if h == 0 else "word_proj")
-                nc.tensor.matmul(forget_proj[:], forget_w[:], looked_up(h * PAIR + s, 1), start=True, stop=True)
-                nc.vector.reduce_sum(a_sum[:, s : s + 1], forget_proj[:], axis=X_AXIS)
-            f_tanh = held.tile([D, PAIR], F32, name=f"f_tanh{h}")
-            nc.scalar.activation(f_tanh[:], a_sum[:], TANH, bias=half_forget_b[:], scale=HALF_MEAN)
-            nc.scalar.activation(f[h][:], f_tanh[:], COPY, bias=HALF_SHARE, scale=HALF_SHARE)
+        a_sum = held.tile([D, R], F32, name="a_sum")
+        f_tanh = held.tile([D, R], F32, name="f_tanh")
+        f = held.tile([D, R], F32, name="f")
+        for group in GATE_GROUPS:
+            for r in group:
+                forget_proj = psum.tile([D, T], F32, name="forget_proj", tag="summed" if r < 2 else "word_proj")
+                nc.tensor.matmul(forget_proj[:], forget_w[:], looked_up(r, 1), start=True, stop=True)
+                nc.vector.reduce_sum(a_sum[:, r : r + 1], forget_proj[:], axis=X_AXIS)
+            of_group = slice(group[0], group[-1] + 1)
+            nc.scalar.activation(f_tanh[:, of_group], a_sum[:, of_group], TANH, bias=half_forget_b[:], scale=HALF_MEAN)
+            nc.scalar.activation(f[:, of_group], f_tanh[:, of_group], COPY, bias=HALF_SHARE, scale=HALF_SHARE)
 
         result = held.tile([D, N], F32, name="result")
         for r in range(R):
-            h, s = divmod(r, PAIR)
             picked = psum.tile([D, T], F32, name="picked", tag="picked", bufs=R)
             nc.tensor.matmul(picked[:], scaled_identity[:], looked_up(r, 1), start=True, stop=True)
             nc.vector.scalar_tensor_tensor(
-                result[:, r * T : (r + 1) * T], share[r][:], f[h][:, s : s + 1], picked[:],
+                result[:, r * T : (r + 1) * T], share[r][:], f[:, r : r + 1], picked[:],
                 op0=ADD, op1=MULT,
             )
             nc.sync.dma_start(out[:, r * T : (r + 1) * T], result[:, r * T : (r + 1) * T])

@@ -26,19 +26,19 @@ def tile_slstm_kernel(tc, table, w_word, w_sent, w_forget, b_word, b_forget, off
         tc.psum_pool(name="psum", bufs=2) as psum,
     ):
         words = held.tile([D, S], BF16, name="words")
-        nc.sync.dma_start(words[:], table)
+        nc.scalar.dma_start(words[:], table)
         offsets = held.tile([D, N // 16], U16, name="offsets")
         nc.sync.dma_start(offsets[:], offs)
         sent_w = held.tile([D, D], BF16, name="sent_w")
-        nc.scalar.dma_start(sent_w[:], w_sent)
+        nc.sync.dma_start(sent_w[:], w_sent)
         word_w = held.tile([D, D], BF16, name="word_w")
-        nc.sync.dma_start(word_w[:], w_word)
+        nc.scalar.dma_start(word_w[:], w_word)
         word_b = held.tile([D, 1], F32, name="word_b")
-        nc.scalar.dma_start(word_b[:], b_word)
+        nc.sync.dma_start(word_b[:], b_word)
         forget_w = held.tile([D, D], BF16, name="forget_w")
-        nc.sync.dma_start(forget_w[:], w_forget)
+        nc.scalar.dma_start(forget_w[:], w_forget)
         forget_b = held.tile([D, 1], F32, name="forget_b")
-        nc.scalar.dma_start(forget_b[:], b_forget)
+        nc.sync.dma_start(forget_b[:], b_forget)
         identity = held.tile([D, D], BF16, name="identity")
         make_identity(nc, identity[:])
         scaled_identity = held.tile([D, D], BF16, name="scaled_identity")

import concourse.mybir as mybir
from concourse.masks import make_identity

D = 128
S = 4096
N = 1024
T = 256
R = N // T
GATE_GROUPS = ((0, 1), (2,), (3,))
HALF_MEAN = 0.5 / T
HALF_SHARE = 0.5 / T
FLOPS = 3 * 2 * D * D * N

BF16, F32, U16 = mybir.dt.bfloat16, mybir.dt.float32, mybir.dt.uint16
MULT, ADD = mybir.AluOpType.mult, mybir.AluOpType.add
TANH, EXP = mybir.ActivationFunctionType.Tanh, mybir.ActivationFunctionType.Exp
COPY = mybir.ActivationFunctionType.Copy
X_AXIS = mybir.AxisListType.X


def tile_slstm_kernel(tc, table, w_word, w_sent, w_forget, b_word, b_forget, offs, out):
    nc = tc.nc
    with (
        tc.tile_pool(name="held", bufs=1) as held,
        tc.tile_pool(name="scratch", bufs=2) as scratch,
        tc.psum_pool(name="psum", bufs=2) as psum,
    ):
        words = held.tile([D, S], BF16, name="words")
        nc.scalar.dma_start(words[:], table)
        offsets = held.tile([D, N // 16], U16, name="offsets")
        nc.sync.dma_start(offsets[:], offs)
        sent_w = held.tile([D, D], BF16, name="sent_w")
        nc.sync.dma_start(sent_w[:], w_sent)
        word_w = held.tile([D, D], BF16, name="word_w")
        nc.scalar.dma_start(word_w[:], w_word)
        word_b = held.tile([D, 1], F32, name="word_b")
        nc.sync.dma_start(word_b[:], b_word)
        forget_w = held.tile([D, D], BF16, name="forget_w")
        nc.scalar.dma_start(forget_w[:], w_forget)
        forget_b = held.tile([D, 1], F32, name="forget_b")
        nc.sync.dma_start(forget_b[:], b_forget)
        identity = held.tile([D, D], BF16, name="identity")
        make_identity(nc, identity[:])
        scaled_identity = held.tile([D, D], BF16, name="scaled_identity")
        nc.gpsimd.tensor_scalar(scaled_identity[:], identity[:], float(T), None, op0=MULT)

        primer = held.tile([D, 1], F32, name="primer")
        nc.vector.memset(primer[:], 0.0)
        primed = held.tile([D, 1], F32, name="primed")
        nc.scalar.activation(primed[:], primer[:], TANH)

        half_word_b = held.tile([D, 1], F32, name="half_word_b")
        nc.vector.tensor_scalar(half_word_b[:], word_b[:], 0.5, None, op0=MULT)
        half_forget_b = held.tile([D, 1], F32, name="half_forget_b")
        nc.vector.tensor_scalar(half_forget_b[:], forget_b[:], 0.5, None, op0=MULT)

        def looked_up(first_sentence, sentences):
            first = first_sentence * T // 16
            return words[:].indirect(offsets[:, first : first + sentences * T // 16])

        gate = [held.tile([D, T], F32, name=f"gate{r}") for r in range(R)]
        x = [held.tile([D, T], F32, name=f"x{r}") for r in range(R)]
        x_sum = [held.tile([D, 1], F32, name=f"x_sum{r}") for r in range(R)]
        x_sum_inv = [held.tile([D, 1], F32, name=f"x_sum_inv{r}") for r in range(R)]
        share = [held.tile([D, T], F32, name=f"share{r}") for r in range(R)]

        def make_share(r):
            nc.scalar.activation(x[r][:], gate[r][:], EXP, scale=0.5, accum_out=x_sum[r][:])
            nc.vector.reciprocal(x_sum_inv[r][:], x_sum[r][:])
            if r == R - 1:
                nc.scalar.activation(share[r][:], x[r][:], COPY, scale=x_sum_inv[r][:])
            else:
                nc.vector.tensor_scalar(share[r][:], x[r][:], x_sum_inv[r][:], None, op0=MULT)

        for r in range(R):
            sent_proj = psum.tile([D, T], F32, name="sent_proj", tag="summed")
            nc.tensor.matmul(sent_proj[:], sent_w[:], looked_up(r, 1), start=True, stop=True)
            word_proj = psum.tile([D, T], F32, name="word_proj", tag="word_proj")
            nc.tensor.matmul(word_proj[:], word_w[:], looked_up(r, 1), start=True, stop=True)

            scaled = scratch.tile([D, T], F32, name="scaled")
            gate_bias = held.tile([D, 1], F32, name=f"gate_bias{r}")
            nc.vector.tensor_scalar(
                scaled[:], sent_proj[:], HALF_MEAN, half_word_b[:],
                op0=MULT, op1=ADD, accum_out=gate_bias[:],
            )
            nc.scalar.activation(gate[r][:], word_proj[:], TANH, bias=gate_bias[:], scale=0.5)
            if r > 0:
                make_share(r - 1)
        make_share(R - 1)

        a_sum = held.tile([D, R], F32, name="a_sum")
        f_tanh = held.tile([D, R], F32, name="f_tanh")
        f = held.tile([D, R], F32, name="f")
        for group in GATE_GROUPS:
            for r in group:
                forget_proj = psum.tile([D, T], F32, name="forget_proj", tag="summed" if r < 2 else "word_proj")
                nc.tensor.matmul(forget_proj[:], forget_w[:], looked_up(r, 1), start=True, stop=True)
                nc.vector.reduce_sum(a_sum[:, r : r + 1], forget_proj[:], axis=X_AXIS)
            of_group = slice(group[0], group[-1] + 1)
            nc.scalar.activation(f_tanh[:, of_group], a_sum[:, of_group], TANH, bias=half_forget_b[:], scale=HALF_MEAN)
            nc.scalar.activation(f[:, of_group], f_tanh[:, of_group], COPY, bias=HALF_SHARE, scale=HALF_SHARE)

        result = held.tile([D, N], F32, name="result")
        for r in range(R):
            picked = psum.tile([D, T], F32, name="picked", tag="picked", bufs=R)
            nc.tensor.matmul(picked[:], scaled_identity[:], looked_up(r, 1), start=True, stop=True)
            nc.vector.scalar_tensor_tensor(
                result[:, r * T : (r + 1) * T], share[r][:], f[:, r : r + 1], picked[:],
                op0=ADD, op1=MULT,
            )
            nc.sync.dma_start(out[:, r * T : (r + 1) * T], result[:, r * T : (r + 1) * T])
